import numpy as np
import ml_dtypes

BF16 = ml_dtypes.bfloat16


def bf(x):
    return np.asarray(x, np.float32).astype(BF16)


def f32(x):
    return np.asarray(x, np.float32)


def f64(x):
    return np.asarray(x).astype(np.float64)


def striped(idx):
    return np.tile(idx.reshape(-1, 16).T, (8, 1))


S, D, F, N = 1024, 128, 384, 512


def setup_inputs():
    return {
        "table": bf(np.random.standard_normal((D, S))),
        "item": bf(np.random.standard_normal((D, N))),
        "txt": bf(np.random.standard_normal((D, N))),
        "w_img": bf(np.random.standard_normal((D, D)) / np.sqrt(D)),
        "b_img": f32(0.1 * np.random.standard_normal((D, 1))),
        "w_txt": bf(np.random.standard_normal((D, D)) / np.sqrt(D)),
        "b_txt": f32(0.1 * np.random.standard_normal((D, 1))),
        "w_fuse": bf(np.random.standard_normal((F, D)) / np.sqrt(F)),
        "b_fuse": f32(0.1 * np.random.standard_normal((D, 1))),
        "offs": striped(np.random.permutation(S)[:N]),
    }


def reference(table, item, txt, w_img, b_img, w_txt, b_txt, w_fuse, b_fuse, offs):
    idx = offs[:16].T.reshape(-1)
    h_img = f64(w_img).T @ f64(table)[:, idx] + f64(b_img)
    h_txt = f64(w_txt).T @ f64(txt) + f64(b_txt)
    return f64(w_fuse).T @ np.concatenate([f64(item), h_img, h_txt], axis=0) + f64(b_fuse)

@@ -1,0 +1,58 @@
+import concourse.mybir as mybir
+
+BF16, F32, U16 = mybir.dt.bfloat16, mybir.dt.float32, mybir.dt.uint16
+ADD = mybir.AluOpType.add
+IDENTITY = mybir.ActivationFunctionType.Identity
+
+P = 128
+S = 1024
+N = 512
+
+FLOPS = 2 * P * P * N * 5
+
+
+def tile_kdsr_kernel(tc, table, item, txt, w_img, b_img, w_txt, b_txt, w_fuse, b_fuse, offs, out):
+    nc = tc.nc
+    with (
+        tc.tile_pool(name="held", bufs=1) as held,
+        tc.psum_pool(name="psum", bufs=1) as psum,
+    ):
+        offsets = held.tile([P, N // 16], U16, name="offsets")
+        nc.sync.dma_start(offsets[:], offs)
+        table_sb = held.tile([P, S], BF16, name="table_sb")
+        nc.sync.dma_start(table_sb[:], table)
+        w_img_sb = held.tile([P, P], BF16, name="w_img_sb")
+        nc.scalar.dma_start(w_img_sb[:], w_img)
+        w_txt_sb = held.tile([P, P], BF16, name="w_txt_sb")
+        nc.scalar.dma_start(w_txt_sb[:], w_txt)
+        txt_sb = held.tile([P, N], BF16, name="txt_sb")
+        nc.scalar.dma_start(txt_sb[:], txt)
+        b_img_sb = held.tile([P, 1], F32, name="b_img_sb")
+        nc.gpsimd.dma_start(b_img_sb[:], b_img)
+        b_txt_sb = held.tile([P, 1], F32, name="b_txt_sb")
+        nc.gpsimd.dma_start(b_txt_sb[:], b_txt)
+        b_fuse_sb = held.tile([P, 1], F32, name="b_fuse_sb")
+        nc.gpsimd.dma_start(b_fuse_sb[:], b_fuse)
+        w_fuse_sb = held.tile([P, 3, P], BF16, name="w_fuse_sb")
+        nc.scalar.dma_start(w_fuse_sb[:], w_fuse.rearrange("(b k) m -> k b m", k=P))
+        item_sb = held.tile([P, N], BF16, name="item_sb")
+        nc.sync.dma_start(item_sb[:], item)
+
+        img_ps = psum.tile([P, N], F32, name="img_ps")
+        nc.tensor.matmul(img_ps[:], w_img_sb[:], table_sb[:].indirect(offsets[:]), start=True, stop=True)
+        txt_ps = psum.tile([P, N], F32, name="txt_ps")
+        nc.tensor.matmul(txt_ps[:], w_txt_sb[:], txt_sb[:], start=True, stop=True)
+
+        h_img = held.tile([P, N], BF16, name="h_img")
+        nc.vector.tensor_scalar(h_img[:], img_ps[:], b_img_sb[:, 0:1], None, ADD)
+        h_txt = held.tile([P, N], BF16, name="h_txt")
+        nc.scalar.activation(h_txt[:], txt_ps[:], IDENTITY, bias=b_txt_sb[:, 0:1])
+
+        out_ps = psum.tile([P, N], F32, name="out_ps")
+        nc.tensor.matmul(out_ps[:], w_fuse_sb[:, 0, :], item_sb[:], start=True, stop=False)
+        nc.tensor.matmul(out_ps[:], w_fuse_sb[:, 1, :], h_img[:], start=False, stop=False)
+        nc.tensor.matmul(out_ps[:], w_fuse_sb[:, 2, :], h_txt[:], start=False, stop=True)
+
+        out_sb = held.tile([P, N], F32, name="out_sb")
+        nc.vector.tensor_scalar(out_sb[:], out_ps[:], b_fuse_sb[:, 0:1], None, ADD)
+        nc.sync.dma_start(out, out_sb[:])

@@ -7,16 +7,29 @@ IDENTITY = mybir.ActivationFunctionType.Identity
 P = 128
 S = 1024
 N = 512
+PIECES = 2
+W = N // PIECES
 
 FLOPS = 2 * P * P * N * 5
 
 
 def tile_kdsr_kernel(tc, table, item, txt, w_img, b_img, w_txt, b_txt, w_fuse, b_fuse, offs, out):
     nc = tc.nc
+
+    def add_bias(piece, result, product, bias):
+        if piece == 0:
+            nc.vector.tensor_scalar(result, product, bias, None, ADD)
+        else:
+            nc.scalar.activation(result, product, IDENTITY, bias=bias)
+
     with (
         tc.tile_pool(name="held", bufs=1) as held,
         tc.psum_pool(name="psum", bufs=1) as psum,
     ):
+        scratch = held.tile([P, 1], F32, name="scratch")
+        nc.vector.memset(scratch[:], 0.0)
+        warmed = held.tile([P, 1], F32, name="warmed")
+
         offsets = held.tile([P, N // 16], U16, name="offsets")
         nc.sync.dma_start(offsets[:], offs)
         table_sb = held.tile([P, S], BF16, name="table_sb")
@@ -28,31 +41,39 @@ def tile_kdsr_kernel(tc, table, item, txt, w_img, b_img, w_txt, b_txt, w_fuse, b
         txt_sb = held.tile([P, N], BF16, name="txt_sb")
         nc.scalar.dma_start(txt_sb[:], txt)
         b_img_sb = held.tile([P, 1], F32, name="b_img_sb")
-        nc.gpsimd.dma_start(b_img_sb[:], b_img)
+        nc.sync.dma_start(b_img_sb[:], b_img)
         b_txt_sb = held.tile([P, 1], F32, name="b_txt_sb")
-        nc.gpsimd.dma_start(b_txt_sb[:], b_txt)
+        nc.scalar.dma_start(b_txt_sb[:], b_txt)
         b_fuse_sb = held.tile([P, 1], F32, name="b_fuse_sb")
-        nc.gpsimd.dma_start(b_fuse_sb[:], b_fuse)
+        nc.sync.dma_start(b_fuse_sb[:], b_fuse)
         w_fuse_sb = held.tile([P, 3, P], BF16, name="w_fuse_sb")
         nc.scalar.dma_start(w_fuse_sb[:], w_fuse.rearrange("(b k) m -> k b m", k=P))
         item_sb = held.tile([P, N], BF16, name="item_sb")
         nc.sync.dma_start(item_sb[:], item)
+        nc.scalar.activation(warmed[:], scratch[:], IDENTITY)
 
-        img_ps = psum.tile([P, N], F32, name="img_ps")
-        nc.tensor.matmul(img_ps[:], w_img_sb[:], table_sb[:].indirect(offsets[:]), start=True, stop=True)
-        txt_ps = psum.tile([P, N], F32, name="txt_ps")
-        nc.tensor.matmul(txt_ps[:], w_txt_sb[:], txt_sb[:], start=True, stop=True)
+        h_img = []
+        for piece in range(PIECES):
+            img_ps = psum.tile([P, W], F32, name=f"img_ps{piece}")
+            picked = table_sb[:].indirect(offsets[:, piece * (W // 16) : (piece + 1) * (W // 16)])
+            nc.tensor.matmul(img_ps[:], w_img_sb[:], picked, start=True, stop=True)
+            h_img.append(held.tile([P, W], BF16, name=f"h_img{piece}"))
+            add_bias(piece, h_img[piece][:], img_ps[:], b_img_sb[:, 0:1])
 
-        h_img = held.tile([P, N], BF16, name="h_img")
-        nc.vector.tensor_scalar(h_img[:], img_ps[:], b_img_sb[:, 0:1], None, ADD)
-        h_txt = held.tile([P, N], BF16, name="h_txt")
-        nc.scalar.activation(h_txt[:], txt_ps[:], IDENTITY, bias=b_txt_sb[:, 0:1])
+        h_txt = []
+        for piece in range(PIECES):
+            txt_ps = psum.tile([P, W], F32, name=f"txt_ps{piece}")
+            nc.tensor.matmul(txt_ps[:], w_txt_sb[:], txt_sb[:, piece * W : (piece + 1) * W], start=True, stop=True)
+            h_txt.append(held.tile([P, W], BF16, name=f"h_txt{piece}"))
+            add_bias(piece, h_txt[piece][:], txt_ps[:], b_txt_sb[:, 0:1])
 
-        out_ps = psum.tile([P, N], F32, name="out_ps")
-        nc.tensor.matmul(out_ps[:], w_fuse_sb[:, 0, :], item_sb[:], start=True, stop=False)
-        nc.tensor.matmul(out_ps[:], w_fuse_sb[:, 1, :], h_img[:], start=False, stop=False)
-        nc.tensor.matmul(out_ps[:], w_fuse_sb[:, 2, :], h_txt[:], start=False, stop=True)
-
-        out_sb = held.tile([P, N], F32, name="out_sb")
-        nc.vector.tensor_scalar(out_sb[:], out_ps[:], b_fuse_sb[:, 0:1], None, ADD)
-        nc.sync.dma_start(out, out_sb[:])
+        for piece in range(PIECES):
+            columns = slice(piece * W, (piece + 1) * W)
+            out_ps = psum.tile([P, W], F32, name=f"out_ps{piece}")
+            nc.tensor.matmul(out_ps[:], w_fuse_sb[:, 0, :], item_sb[:, columns], start=True, stop=False)
+            nc.tensor.matmul(out_ps[:], w_fuse_sb[:, 1, :], h_img[piece][:], start=False, stop=False)
+            nc.tensor.matmul(out_ps[:], w_fuse_sb[:, 2, :], h_txt[piece][:], start=False, stop=True)
+            out_sb = held.tile([P, W], F32, name=f"out_sb{piece}")
+            add_bias(piece, out_sb[:], out_ps[:], b_fuse_sb[:, 0:1])
+            store_queue = nc.sync if piece == 0 else nc.scalar
+            store_queue.dma_start(out[:, columns], out_sb[:])

@@ -9,6 +9,7 @@ S = 1024
 N = 512
 PIECES = 2
 W = N // PIECES
+WARM_UPS = 5
 
 FLOPS = 2 * P * P * N * 5
 
@@ -29,6 +30,12 @@ def tile_kdsr_kernel(tc, table, item, txt, w_img, b_img, w_txt, b_txt, w_fuse, b
         scratch = held.tile([P, 1], F32, name="scratch")
         nc.vector.memset(scratch[:], 0.0)
         warmed = held.tile([P, 1], F32, name="warmed")
+
+        zeros = held.tile([P, N], BF16, name="zeros")
+        nc.vector.memset(zeros[:], 0.0)
+        unread_ps = psum.tile([P, N], F32, name="unread_ps")
+        for warm_up in range(WARM_UPS):
+            nc.tensor.matmul(unread_ps[:], zeros[:, 0:P], zeros[:], start=True, stop=True)
 
         offsets = held.tile([P, N // 16], U16, name="offsets")
         nc.sync.dma_start(offsets[:], offs)

@@ -39,25 +39,25 @@ def tile_kdsr_kernel(tc, table, item, txt, w_img, b_img, w_txt, b_txt, w_fuse, b
 
         offsets = held.tile([P, N // 16], U16, name="offsets")
         nc.sync.dma_start(offsets[:], offs)
-        table_sb = held.tile([P, S], BF16, name="table_sb")
-        nc.sync.dma_start(table_sb[:], table)
         w_img_sb = held.tile([P, P], BF16, name="w_img_sb")
-        nc.scalar.dma_start(w_img_sb[:], w_img)
-        w_txt_sb = held.tile([P, P], BF16, name="w_txt_sb")
-        nc.scalar.dma_start(w_txt_sb[:], w_txt)
-        txt_sb = held.tile([P, N], BF16, name="txt_sb")
-        nc.scalar.dma_start(txt_sb[:], txt)
+        nc.sync.dma_start(w_img_sb[:], w_img)
         b_img_sb = held.tile([P, 1], F32, name="b_img_sb")
-        nc.sync.dma_start(b_img_sb[:], b_img)
+        nc.scalar.dma_start(b_img_sb[:], b_img)
         b_txt_sb = held.tile([P, 1], F32, name="b_txt_sb")
         nc.scalar.dma_start(b_txt_sb[:], b_txt)
         b_fuse_sb = held.tile([P, 1], F32, name="b_fuse_sb")
-        nc.sync.dma_start(b_fuse_sb[:], b_fuse)
+        nc.scalar.dma_start(b_fuse_sb[:], b_fuse)
+        nc.scalar.activation(warmed[:], scratch[:], IDENTITY)
+        table_sb = held.tile([P, S], BF16, name="table_sb")
+        nc.sync.dma_start(table_sb[:], table)
+        w_txt_sb = held.tile([P, P], BF16, name="w_txt_sb")
+        nc.sync.dma_start(w_txt_sb[:], w_txt)
+        txt_sb = held.tile([P, N], BF16, name="txt_sb")
+        nc.sync.dma_start(txt_sb[:], txt)
         w_fuse_sb = held.tile([P, 3, P], BF16, name="w_fuse_sb")
-        nc.scalar.dma_start(w_fuse_sb[:], w_fuse.rearrange("(b k) m -> k b m", k=P))
+        nc.sync.dma_start(w_fuse_sb[:], w_fuse.rearrange("(b k) m -> k b m", k=P))
         item_sb = held.tile([P, N], BF16, name="item_sb")
         nc.sync.dma_start(item_sb[:], item)
-        nc.scalar.activation(warmed[:], scratch[:], IDENTITY)
 
         h_img = []
         for piece in range(PIECES):

@@ -9,6 +9,7 @@ S = 1024
 N = 512
 PIECES = 2
 W = N // PIECES
+BLOCK = 32
 WARM_UPS = 5
 
 FLOPS = 2 * P * P * N * 5
@@ -31,6 +32,9 @@ def tile_kdsr_kernel(tc, table, item, txt, w_img, b_img, w_txt, b_txt, w_fuse, b
         nc.vector.memset(scratch[:], 0.0)
         warmed = held.tile([P, 1], F32, name="warmed")
 
+        bias_rows = held.tile([P, 4 * BLOCK], F32, name="bias_rows", align_bytes=64)
+        nc.gpsimd.memset(bias_rows[:], 0.0)
+
         zeros = held.tile([P, N], BF16, name="zeros")
         nc.vector.memset(zeros[:], 0.0)
         unread_ps = psum.tile([P, N], F32, name="unread_ps")
@@ -41,12 +45,11 @@ def tile_kdsr_kernel(tc, table, item, txt, w_img, b_img, w_txt, b_txt, w_fuse, b
         nc.sync.dma_start(offsets[:], offs)
         w_img_sb = held.tile([P, P], BF16, name="w_img_sb")
         nc.sync.dma_start(w_img_sb[:], w_img)
-        b_img_sb = held.tile([P, 1], F32, name="b_img_sb")
-        nc.scalar.dma_start(b_img_sb[:], b_img)
-        b_txt_sb = held.tile([P, 1], F32, name="b_txt_sb")
-        nc.scalar.dma_start(b_txt_sb[:], b_txt)
-        b_fuse_sb = held.tile([P, 1], F32, name="b_fuse_sb")
-        nc.scalar.dma_start(b_fuse_sb[:], b_fuse)
+        for i, bias in enumerate((b_img, b_txt, b_fuse)):
+            nc.scalar.dma_start(bias_rows[0:P:BLOCK, i * BLOCK : (i + 1) * BLOCK], bias.rearrange("(r c) o -> r (c o)", c=BLOCK))
+        bias_columns = held.tile([P, 4 * BLOCK], F32, name="bias_columns", align_bytes=64)
+        nc.vector.transpose(bias_columns[:], bias_rows[:])
+        b_img_sb, b_txt_sb, b_fuse_sb = (bias_columns[:, i * BLOCK : i * BLOCK + 1] for i in range(3))
         nc.scalar.activation(warmed[:], scratch[:], IDENTITY)
         table_sb = held.tile([P, S], BF16, name="table_sb")
         nc.sync.dma_start(table_sb[:], table)
@@ -65,14 +68,14 @@ def tile_kdsr_kernel(tc, table, item, txt, w_img, b_img, w_txt, b_txt, w_fuse, b
             picked = table_sb[:].indirect(offsets[:, piece * (W // 16) : (piece + 1) * (W // 16)])
             nc.tensor.matmul(img_ps[:], w_img_sb[:], picked, start=True, stop=True)
             h_img.append(held.tile([P, W], BF16, name=f"h_img{piece}"))
-            add_bias(piece, h_img[piece][:], img_ps[:], b_img_sb[:, 0:1])
+            add_bias(piece, h_img[piece][:], img_ps[:], b_img_sb)
 
         h_txt = []
         for piece in range(PIECES):
             txt_ps = psum.tile([P, W], F32, name=f"txt_ps{piece}")
             nc.tensor.matmul(txt_ps[:], w_txt_sb[:], txt_sb[:, piece * W : (piece + 1) * W], start=True, stop=True)
             h_txt.append(held.tile([P, W], BF16, name=f"h_txt{piece}"))
-            add_bias(piece, h_txt[piece][:], txt_ps[:], b_txt_sb[:, 0:1])
+            add_bias(piece, h_txt[piece][:], txt_ps[:], b_txt_sb)
 
         for piece in range(PIECES):
             columns = slice(piece * W, (piece + 1) * W)
@@ -81,6 +84,6 @@ def tile_kdsr_kernel(tc, table, item, txt, w_img, b_img, w_txt, b_txt, w_fuse, b
             nc.tensor.matmul(out_ps[:], w_fuse_sb[:, 1, :], h_img[piece][:], start=False, stop=False)
             nc.tensor.matmul(out_ps[:], w_fuse_sb[:, 2, :], h_txt[piece][:], start=False, stop=True)
             out_sb = held.tile([P, W], F32, name=f"out_sb{piece}")
-            add_bias(piece, out_sb[:], out_ps[:], b_fuse_sb[:, 0:1])
+            add_bias(piece, out_sb[:], out_ps[:], b_fuse_sb)
             store_queue = nc.sync if piece == 0 else nc.scalar
             store_queue.dma_start(out[:, columns], out_sb[:])

@@ -28,10 +28,6 @@ def tile_kdsr_kernel(tc, table, item, txt, w_img, b_img, w_txt, b_txt, w_fuse, b
         tc.tile_pool(name="held", bufs=1) as held,
         tc.psum_pool(name="psum", bufs=1) as psum,
     ):
-        scratch = held.tile([P, 1], F32, name="scratch")
-        nc.vector.memset(scratch[:], 0.0)
-        warmed = held.tile([P, 1], F32, name="warmed")
-
         bias_rows = held.tile([P, 4 * BLOCK], F32, name="bias_rows", align_bytes=64)
         nc.gpsimd.memset(bias_rows[:], 0.0)
 
@@ -50,7 +46,8 @@ def tile_kdsr_kernel(tc, table, item, txt, w_img, b_img, w_txt, b_txt, w_fuse, b
         bias_columns = held.tile([P, 4 * BLOCK], F32, name="bias_columns", align_bytes=64)
         nc.vector.transpose(bias_columns[:], bias_rows[:])
         b_img_sb, b_txt_sb, b_fuse_sb = (bias_columns[:, i * BLOCK : i * BLOCK + 1] for i in range(3))
-        nc.scalar.activation(warmed[:], scratch[:], IDENTITY)
+        warmed = held.tile([P, 1], F32, name="warmed")
+        nc.scalar.activation(warmed[:], bias_rows[:, 3 * BLOCK : 3 * BLOCK + 1], IDENTITY)
         table_sb = held.tile([P, S], BF16, name="table_sb")
         nc.sync.dma_start(table_sb[:], table)
         w_txt_sb = held.tile([P, P], BF16, name="w_txt_sb")

@@ -29,7 +29,10 @@ def tile_kdsr_kernel(tc, table, item, txt, w_img, b_img, w_txt, b_txt, w_fuse, b
         tc.psum_pool(name="psum", bufs=1) as psum,
     ):
         bias_rows = held.tile([P, 4 * BLOCK], F32, name="bias_rows", align_bytes=64)
-        nc.gpsimd.memset(bias_rows[:], 0.0)
+        nc.vector.memset(bias_rows[:], 0.0)
+
+        warmed = held.tile([P, 1], F32, name="warmed")
+        nc.scalar.activation(warmed[:], bias_rows[:, 3 * BLOCK : 3 * BLOCK + 1], IDENTITY)
 
         zeros = held.tile([P, N], BF16, name="zeros")
         nc.vector.memset(zeros[:], 0.0)
@@ -41,15 +44,13 @@ def tile_kdsr_kernel(tc, table, item, txt, w_img, b_img, w_txt, b_txt, w_fuse, b
         nc.sync.dma_start(offsets[:], offs)
         w_img_sb = held.tile([P, P], BF16, name="w_img_sb")
         nc.sync.dma_start(w_img_sb[:], w_img)
+        table_sb = held.tile([P, S], BF16, name="table_sb")
+        nc.sync.dma_start(table_sb[:], table)
         for i, bias in enumerate((b_img, b_txt, b_fuse)):
-            nc.scalar.dma_start(bias_rows[0:P:BLOCK, i * BLOCK : (i + 1) * BLOCK], bias.rearrange("(r c) o -> r (c o)", c=BLOCK))
+            nc.sync.dma_start(bias_rows[0:P:BLOCK, i * BLOCK : (i + 1) * BLOCK], bias.rearrange("(r c) o -> r (c o)", c=BLOCK))
         bias_columns = held.tile([P, 4 * BLOCK], F32, name="bias_columns", align_bytes=64)
         nc.vector.transpose(bias_columns[:], bias_rows[:])
         b_img_sb, b_txt_sb, b_fuse_sb = (bias_columns[:, i * BLOCK : i * BLOCK + 1] for i in range(3))
-        warmed = held.tile([P, 1], F32, name="warmed")
-        nc.scalar.activation(warmed[:], bias_rows[:, 3 * BLOCK : 3 * BLOCK + 1], IDENTITY)
-        table_sb = held.tile([P, S], BF16, name="table_sb")
-        nc.sync.dma_start(table_sb[:], table)
         w_txt_sb = held.tile([P, P], BF16, name="w_txt_sb")
         nc.sync.dma_start(w_txt_sb[:], w_txt)
         txt_sb = held.tile([P, N], BF16, name="txt_sb")

@@ -10,7 +10,7 @@ N = 512
 PIECES = 2
 W = N // PIECES
 BLOCK = 32
-WARM_UPS = 5
+WARM_UPS = 4
 
 FLOPS = 2 * P * P * N * 5
 
@@ -28,17 +28,17 @@ def tile_kdsr_kernel(tc, table, item, txt, w_img, b_img, w_txt, b_txt, w_fuse, b
         tc.tile_pool(name="held", bufs=1) as held,
         tc.psum_pool(name="psum", bufs=1) as psum,
     ):
+        zeros = held.tile([P, P], BF16, name="zeros")
+        nc.vector.memset(zeros[:], 0.0)
+        unread_ps = psum.tile([P, N], F32, name="unread_ps")
+        for warm_up in range(WARM_UPS):
+            nc.tensor.matmul(unread_ps[:], zeros[:], zeros[:, 0:1].to_broadcast([P, N]), start=True, stop=True)
+
         bias_rows = held.tile([P, 4 * BLOCK], F32, name="bias_rows", align_bytes=64)
         nc.vector.memset(bias_rows[:], 0.0)
 
         warmed = held.tile([P, 1], F32, name="warmed")
         nc.scalar.activation(warmed[:], bias_rows[:, 3 * BLOCK : 3 * BLOCK + 1], IDENTITY)
-
-        zeros = held.tile([P, N], BF16, name="zeros")
-        nc.vector.memset(zeros[:], 0.0)
-        unread_ps = psum.tile([P, N], F32, name="unread_ps")
-        for warm_up in range(WARM_UPS):
-            nc.tensor.matmul(unread_ps[:], zeros[:, 0:P], zeros[:], start=True, stop=True)
 
         offsets = held.tile([P, N // 16], U16, name="offsets")
         nc.sync.dma_start(offsets[:], offs)

import concourse.mybir as mybir

BF16, F32, U16 = mybir.dt.bfloat16, mybir.dt.float32, mybir.dt.uint16
ADD = mybir.AluOpType.add
IDENTITY = mybir.ActivationFunctionType.Identity

P = 128
S = 1024
N = 512
PIECES = 2
W = N // PIECES
BLOCK = 32
WARM_UPS = 4

FLOPS = 2 * P * P * N * 5


def tile_kdsr_kernel(tc, table, item, txt, w_img, b_img, w_txt, b_txt, w_fuse, b_fuse, offs, out):
    nc = tc.nc

    def add_bias(piece, result, product, bias):
        if piece == 0:
            nc.vector.tensor_scalar(result, product, bias, None, ADD)
        else:
            nc.scalar.activation(result, product, IDENTITY, bias=bias)

    with (
        tc.tile_pool(name="held", bufs=1) as held,
        tc.psum_pool(name="psum", bufs=1) as psum,
    ):
        zeros = held.tile([P, P], BF16, name="zeros")
        nc.vector.memset(zeros[:], 0.0)
        unread_ps = psum.tile([P, N], F32, name="unread_ps")
        for warm_up in range(WARM_UPS):
            nc.tensor.matmul(unread_ps[:], zeros[:], zeros[:, 0:1].to_broadcast([P, N]), start=True, stop=True)

        bias_rows = held.tile([P, 4 * BLOCK], F32, name="bias_rows", align_bytes=64)
        nc.vector.memset(bias_rows[:], 0.0)

        warmed = held.tile([P, 1], F32, name="warmed")
        nc.scalar.activation(warmed[:], bias_rows[:, 3 * BLOCK : 3 * BLOCK + 1], IDENTITY)

        offsets = held.tile([P, N // 16], U16, name="offsets")
        nc.sync.dma_start(offsets[:], offs)
        w_img_sb = held.tile([P, P], BF16, name="w_img_sb")
        nc.sync.dma_start(w_img_sb[:], w_img)
        table_sb = held.tile([P, S], BF16, name="table_sb")
        nc.sync.dma_start(table_sb[:], table)
        for i, bias in enumerate((b_img, b_txt, b_fuse)):
            nc.sync.dma_start(bias_rows[0:P:BLOCK, i * BLOCK : (i + 1) * BLOCK], bias.rearrange("(r c) o -> r (c o)", c=BLOCK))
        bias_columns = held.tile([P, 4 * BLOCK], F32, name="bias_columns", align_bytes=64)
        nc.vector.transpose(bias_columns[:], bias_rows[:])
        b_img_sb, b_txt_sb, b_fuse_sb = (bias_columns[:, i * BLOCK : i * BLOCK + 1] for i in range(3))
        w_txt_sb = held.tile([P, P], BF16, name="w_txt_sb")
        nc.sync.dma_start(w_txt_sb[:], w_txt)
        txt_sb = held.tile([P, N], BF16, name="txt_sb")
        nc.sync.dma_start(txt_sb[:], txt)
        w_fuse_sb = held.tile([P, 3, P], BF16, name="w_fuse_sb")
        nc.sync.dma_start(w_fuse_sb[:], w_fuse.rearrange("(b k) m -> k b m", k=P))
        item_sb = held.tile([P, N], BF16, name="item_sb")
        nc.sync.dma_start(item_sb[:], item)

        h_img = []
        for piece in range(PIECES):
            img_ps = psum.tile([P, W], F32, name=f"img_ps{piece}")
            picked = table_sb[:].indirect(offsets[:, piece * (W // 16) : (piece + 1) * (W // 16)])
            nc.tensor.matmul(img_ps[:], w_img_sb[:], picked, start=True, stop=True)
            h_img.append(held.tile([P, W], BF16, name=f"h_img{piece}"))
            add_bias(piece, h_img[piece][:], img_ps[:], b_img_sb)

        h_txt = []
        for piece in range(PIECES):
            txt_ps = psum.tile([P, W], F32, name=f"txt_ps{piece}")
            nc.tensor.matmul(txt_ps[:], w_txt_sb[:], txt_sb[:, piece * W : (piece + 1) * W], start=True, stop=True)
            h_txt.append(held.tile([P, W], BF16, name=f"h_txt{piece}"))
            add_bias(piece, h_txt[piece][:], txt_ps[:], b_txt_sb)

        for piece in range(PIECES):
            columns = slice(piece * W, (piece + 1) * W)
            out_ps = psum.tile([P, W], F32, name=f"out_ps{piece}")
            nc.tensor.matmul(out_ps[:], w_fuse_sb[:, 0, :], item_sb[:, columns], start=True, stop=False)
            nc.tensor.matmul(out_ps[:], w_fuse_sb[:, 1, :], h_img[piece][:], start=False, stop=False)
            nc.tensor.matmul(out_ps[:], w_fuse_sb[:, 2, :], h_txt[piece][:], start=False, stop=True)
            out_sb = held.tile([P, W], F32, name=f"out_sb{piece}")
            add_bias(piece, out_sb[:], out_ps[:], b_fuse_sb)
            store_queue = nc.sync if piece == 0 else nc.scalar
            store_queue.dma_start(out[:, columns], out_sb[:])
